import numpy as np
import ml_dtypes


def mxq(x, axis, fmt="e4m3"):
    dtype, down = {"e4m3": (ml_dtypes.float8_e4m3fn, 7), "e5m2": (ml_dtypes.float8_e5m2, 14)}[fmt]
    v = np.moveaxis(np.asarray(x, np.float32).astype(ml_dtypes.bfloat16).astype(np.float64), axis, -1)
    blocks = v.reshape(v.shape[:-1] + (-1, 32))
    amax = np.abs(blocks).max(-1, keepdims=True)
    byte = np.maximum(np.where(amax > 0, np.frexp(amax)[1] - 1 + 127, 0) - down, 1)
    scale = np.exp2(byte - 127.0)
    codes = (blocks / scale).astype(np.float32).astype(dtype).astype(np.float64)
    return np.moveaxis((codes * scale).reshape(v.shape), -1, axis)


WIDE = False


def mx_kscale(k):
    if not WIDE:
        return np.ones(k)
    levels = np.array([10, -10, 5, -5, 0])
    a = np.random.permutation(np.resize(levels, k // 512 * 4)).reshape(k // 512, 4)
    idx = np.arange(k)
    return np.exp2(a[idx // 512, idx % 128 // 32])


BF16 = ml_dtypes.bfloat16


def bf(x):
    return np.asarray(x, np.float32).astype(BF16)


def f64(x):
    return np.asarray(x).astype(np.float64)


B, L, F, D, N = 16, 32, 16384, 512, 8192
TOP = 0.8 * np.sqrt(2.0 * np.log(L))


def elu(v):
    return np.where(v > 0.0, v, np.exp(np.minimum(v, 0.0)) - 1.0)


def setup_inputs():
    s = mx_kscale(F)
    return {"x": bf(np.random.standard_normal((B, L, F)) * s),
            "conv_w": bf(np.random.standard_normal((D, F)) / np.sqrt(F) / s),
            "conv_b": bf(np.random.standard_normal(D) * 2.0 - TOP)}


def reference(x, conv_w, conv_b):
    z = (mxq(f64(x), 2, "e4m3") @ mxq(f64(conv_w), 1, "e4m3").T) + f64(conv_b)
    return elu(z).max(axis=1)

@@ -1,0 +1,193 @@
+from contextlib import ExitStack
+
+import concourse.mybir as mybir
+from concourse.masks import make_identity
+
+F32 = mybir.dt.float32
+BF16 = mybir.dt.bfloat16
+U32 = mybir.dt.uint32
+U8 = mybir.dt.uint8
+FP8X4 = mybir.dt.float8_e4m3fn_x4
+ALU = mybir.AluOpType
+
+P = 128
+PACK = 4
+K_PASS = P * PACK
+WORDS_PASS = K_PASS // 2
+
+SEQS, POSITIONS, FEATURES, D_OUT = 16, 32, 16384, 512
+ROWS = SEQS * POSITIONS
+ROW_TILES = ROWS // P
+D_TILES = D_OUT // P
+PASSES = FEATURES // K_PASS
+
+GROUP = 2
+GROUPS = PASSES // GROUP
+LOAD_PASSES = 2
+LOAD_K = LOAD_PASSES * K_PASS
+LOADS = PASSES // LOAD_PASSES
+RAW_BUFS = 6
+
+BANK_WORDS = 512
+BANK_ROWS = BANK_WORDS // 2
+
+FLOPS = 2 * ROWS * D_OUT * FEATURES
+
+assert ROWS == D_OUT and LOAD_PASSES % GROUP == 0
+
+
+def tile_conceptembedmodel_pa_k_kernel(tc, x, conv_w, conv_b, out):
+    nc = tc.nc
+    x_rows = x.rearrange("b l f -> (b l) f").rearrange("(t p) f -> p t f", p=P)
+    w_rows = conv_w.rearrange("(t p) f -> p t f", p=P)
+
+    with ExitStack() as ctx:
+        ctx.enter_context(tc.manual_schedule())
+        const = ctx.enter_context(tc.tile_pool(name="const", bufs=1))
+        raw = ctx.enter_context(tc.tile_pool(name="raw", bufs=RAW_BUFS))
+        stage = ctx.enter_context(tc.tile_pool(name="stage", bufs=3))
+        quantised = ctx.enter_context(tc.tile_pool(name="quantised", bufs=2))
+        z_banks = ctx.enter_context(tc.psum_pool(name="z_banks", bufs=1))
+        t_banks = ctx.enter_context(tc.psum_pool(name="t_banks", bufs=4))
+
+        def load(i):
+            features = slice(i * LOAD_K, (i + 1) * LOAD_K)
+            x_raw = raw.tile([P, ROW_TILES * LOAD_K], BF16, tag="x_raw")
+            nc.sync.dma_start(
+                out=x_raw[:].rearrange("p (t k) -> p t k", t=ROW_TILES), in_=x_rows[:, :, features]
+            )
+            w_raw = raw.tile([P, ROW_TILES * LOAD_K], BF16, tag="w_raw")
+            nc.sync.dma_start(
+                out=w_raw[:].rearrange("p (t k) -> p t k", t=ROW_TILES), in_=w_rows[:, :, features]
+            )
+            return x_raw, w_raw
+
+        def transpose_and_quantise(raw_tile, first_pass_in_load, first_bank, codes, scales):
+            words = raw_tile[:].bitcast(F32)
+            grouped = stage.tile([P, GROUP * ROWS * PACK], BF16, tag="grouped", align_bytes=64)
+            grouped_words = grouped[:].bitcast(F32)
+            for i in range(GROUP):
+                for half in range(ROWS // BANK_ROWS):
+                    bank = t_banks.tile([P, 2, BANK_ROWS], F32, tag="bank")
+                    for u in range(2):
+                        for j in range(BANK_ROWS // P):
+                            t = half * (BANK_ROWS // P) + j
+                            first_word = t * (LOAD_K // 2) + (first_pass_in_load + i) * WORDS_PASS + u * P
+                            nc.tensor.transpose(
+                                out=bank[:, u, j * P : (j + 1) * P],
+                                in_=words[:, first_word : first_word + P],
+                                identity=identity[:],
+                            )
+                    first = (i * ROWS + half * BANK_ROWS) * 2
+                    side_by_side = grouped_words[:, first : first + BANK_WORDS].rearrange("p (r u) -> p r u", u=2)
+                    planes = bank[:].rearrange("p u r -> p r u")
+                    if (first_bank + i * (ROWS // BANK_ROWS) + half) % 4 == 2:
+                        nc.vector.tensor_copy(out=side_by_side, in_=planes)
+                    else:
+                        nc.scalar.copy(out=side_by_side, in_=planes)
+            for i in range(GROUP):
+                nc.vector.quantize_mx(
+                    out=codes[:, i * ROWS : (i + 1) * ROWS].bitcast(FP8X4),
+                    scales=scales[:, i * ROWS : (i + 1) * ROWS],
+                    in_=grouped[:, i * ROWS * PACK : (i + 1) * ROWS * PACK],
+                )
+
+        def prepare(g):
+            x_raw, w_raw = loaded[(g * GROUP) // LOAD_PASSES]
+            first_pass_in_load = (g * GROUP) % LOAD_PASSES
+            banks_per_operand = GROUP * (ROWS // BANK_ROWS)
+            x_codes = quantised.tile([P, GROUP * ROWS], U32, tag="x_codes", align_bytes=64)
+            x_scales = quantised.tile([P, GROUP * ROWS], U8, tag="x_scales", align_bytes=64)
+            transpose_and_quantise(x_raw, first_pass_in_load, 0, x_codes, x_scales)
+            w_codes = quantised.tile([P, GROUP * ROWS], U32, tag="w_codes", align_bytes=64)
+            w_scales = quantised.tile([P, GROUP * ROWS], U8, tag="w_scales", align_bytes=64)
+            transpose_and_quantise(w_raw, first_pass_in_load, banks_per_operand, w_codes, w_scales)
+            return x_codes, x_scales, w_codes, w_scales
+
+        def multiply(g, mx_tiles):
+            x_codes, x_scales, w_codes, w_scales = mx_tiles
+            for m in range(D_TILES):
+                for i in range(GROUP):
+                    c = g * GROUP + i
+                    x_cols = slice(i * ROWS, (i + 1) * ROWS)
+                    w_cols = slice(i * ROWS + m * P, i * ROWS + (m + 1) * P)
+                    nc.tensor.matmul_mx(
+                        out=z[m][:],
+                        lhsT=w_codes[:, w_cols].bitcast(FP8X4),
+                        lhsT_scale=w_scales[:, w_cols],
+                        rhs=x_codes[:, x_cols].bitcast(FP8X4),
+                        rhs_scale=x_scales[:, x_cols],
+                        start=(c == 0),
+                        stop=(c == PASSES - 1),
+                    )
+
+        loaded = {}
+        for i in range(RAW_BUFS):
+            loaded[i] = load(i)
+
+        identity = const.tile([P, P], F32)
+        make_identity(nc, identity[:])
+        bias_rows = const.tile([P, P], BF16)
+        nc.vector.memset(bias_rows[:], 0.0)
+        nc.scalar.dma_start(out=bias_rows[0:D_TILES, :], in_=conv_b.rearrange("(m d) -> m d", m=D_TILES))
+        warm = const.tile([P, 1], F32)
+        nc.vector.memset(warm[:], 0.0)
+        nc.scalar.activation(out=warm[:], in_=warm[:], func=mybir.ActivationFunctionType.Exp)
+        result = const.tile([P, P], F32)
+        nc.vector.memset(result[:], 0.0)
+
+        z = [z_banks.tile([P, ROWS], F32, name="z%d" % m) for m in range(D_TILES)]
+
+        mx_tiles = {}
+        for g in range(GROUPS):
+            mx_tiles[g] = prepare(g)
+            last_group_of_load = (g + 1) * GROUP % LOAD_PASSES == 0
+            next_load = (g * GROUP) // LOAD_PASSES + RAW_BUFS
+            if last_group_of_load and next_load < LOADS:
+                loaded[next_load] = load(next_load)
+            if g == 0:
+                bias_rows_f32 = const.tile([P, P], F32)
+                nc.vector.tensor_copy(out=bias_rows_f32[:], in_=bias_rows[:])
+                bias_bank = t_banks.tile([P, 2, BANK_ROWS], F32, tag="bank")
+                nc.tensor.transpose(out=bias_bank[:, 0, 0:P], in_=bias_rows_f32[:], identity=identity[:])
+                bias = const.tile([P, D_TILES], F32)
+                nc.vector.tensor_copy(out=bias[:], in_=bias_bank[:, 0, 0:D_TILES])
+            else:
+                multiply(g - 1, mx_tiles[g - 1])
+        multiply(GROUPS - 1, mx_tiles[GROUPS - 1])
+
+        z_max = const.tile([P, SEQS * D_TILES], F32)
+        for m in range(D_TILES):
+            nc.vector.tensor_reduce(
+                out=z_max[:].rearrange("p (b m) -> p b m", m=D_TILES)[:, :, m],
+                in_=z[m][:].rearrange("p (b l) -> p b l", l=POSITIONS),
+                axis=mybir.AxisListType.X,
+                op=ALU.max,
+            )
+        v = const.tile([P, SEQS * D_TILES], F32)
+        nc.vector.tensor_tensor(
+            out=v[:].rearrange("p (b m) -> p b m", m=D_TILES),
+            in0=z_max[:].rearrange("p (b m) -> p b m", m=D_TILES),
+            in1=bias[:].unsqueeze(1).to_broadcast([P, SEQS, D_TILES]),
+            op=ALU.add,
+        )
+        negative = const.tile([P, SEQS * D_TILES], F32)
+        nc.vector.tensor_scalar_min(out=negative[:], in0=v[:], scalar1=0.0)
+        exp_negative = const.tile([P, SEQS * D_TILES], F32)
+        nc.scalar.activation(out=exp_negative[:], in_=negative[:], func=mybir.ActivationFunctionType.Exp)
+        positive = const.tile([P, SEQS * D_TILES], F32)
+        nc.vector.tensor_scalar_max(out=positive[:], in0=v[:], scalar1=0.0)
+        nc.vector.scalar_tensor_tensor(
+            out=result[:, 0 : SEQS * D_TILES],
+            in0=exp_negative[:],
+            scalar=-1.0,
+            in1=positive[:],
+            op0=ALU.add,
+            op1=ALU.add,
+        )
+
+        result_bank = t_banks.tile([P, 2, BANK_ROWS], F32, tag="bank")
+        nc.tensor.transpose(out=result_bank[:, 0, 0:P], in_=result[:], identity=identity[:])
+        out_rows = const.tile([SEQS * D_TILES, P], F32)
+        nc.vector.tensor_copy(out=out_rows[:], in_=result_bank[0 : SEQS * D_TILES, 0, 0:P])
+        nc.sync.dma_start(out=out.rearrange("b (m d) -> (b m) d", m=D_TILES), in_=out_rows[:])

@@ -21,7 +21,7 @@ ROW_TILES = ROWS // P
 D_TILES = D_OUT // P
 PASSES = FEATURES // K_PASS
 
-GROUP = 2
+GROUP = 1
 GROUPS = PASSES // GROUP
 LOAD_PASSES = 2
 LOAD_K = LOAD_PASSES * K_PASS

@@ -21,7 +21,7 @@ ROW_TILES = ROWS // P
 D_TILES = D_OUT // P
 PASSES = FEATURES // K_PASS
 
-GROUP = 1
+GROUP = 2
 GROUPS = PASSES // GROUP
 LOAD_PASSES = 2
 LOAD_K = LOAD_PASSES * K_PASS
@@ -62,7 +62,7 @@ def tile_conceptembedmodel_pa_k_kernel(tc, x, conv_w, conv_b, out):
             )
             return x_raw, w_raw
 
-        def transpose_and_quantise(raw_tile, first_pass_in_load, first_bank, codes, scales):
+        def transpose_and_quantise(raw_tile, first_pass_in_load, vector_helps, codes, scales):
             words = raw_tile[:].bitcast(F32)
             grouped = stage.tile([P, GROUP * ROWS * PACK], BF16, tag="grouped", align_bytes=64)
             grouped_words = grouped[:].bitcast(F32)
@@ -81,7 +81,7 @@ def tile_conceptembedmodel_pa_k_kernel(tc, x, conv_w, conv_b, out):
                     first = (i * ROWS + half * BANK_ROWS) * 2
                     side_by_side = grouped_words[:, first : first + BANK_WORDS].rearrange("p (r u) -> p r u", u=2)
                     planes = bank[:].rearrange("p u r -> p r u")
-                    if (first_bank + i * (ROWS // BANK_ROWS) + half) % 4 == 2:
+                    if vector_helps and half == 1:
                         nc.vector.tensor_copy(out=side_by_side, in_=planes)
                     else:
                         nc.scalar.copy(out=side_by_side, in_=planes)
@@ -95,13 +95,12 @@ def tile_conceptembedmodel_pa_k_kernel(tc, x, conv_w, conv_b, out):
         def prepare(g):
             x_raw, w_raw = loaded[(g * GROUP) // LOAD_PASSES]
             first_pass_in_load = (g * GROUP) % LOAD_PASSES
-            banks_per_operand = GROUP * (ROWS // BANK_ROWS)
             x_codes = quantised.tile([P, GROUP * ROWS], U32, tag="x_codes", align_bytes=64)
             x_scales = quantised.tile([P, GROUP * ROWS], U8, tag="x_scales", align_bytes=64)
-            transpose_and_quantise(x_raw, first_pass_in_load, 0, x_codes, x_scales)
+            transpose_and_quantise(x_raw, first_pass_in_load, True, x_codes, x_scales)
             w_codes = quantised.tile([P, GROUP * ROWS], U32, tag="w_codes", align_bytes=64)
             w_scales = quantised.tile([P, GROUP * ROWS], U8, tag="w_scales", align_bytes=64)
-            transpose_and_quantise(w_raw, first_pass_in_load, banks_per_operand, w_codes, w_scales)
+            transpose_and_quantise(w_raw, first_pass_in_load, False, w_codes, w_scales)
             return x_codes, x_scales, w_codes, w_scales
 
         def multiply(g, mx_tiles):

@@ -26,6 +26,7 @@ GROUPS = PASSES // GROUP
 LOAD_PASSES = 2
 LOAD_K = LOAD_PASSES * K_PASS
 LOADS = PASSES // LOAD_PASSES
+BIAS_GROUP = 4
 RAW_BUFS = 6
 
 BANK_WORDS = 512
@@ -64,7 +65,7 @@ def tile_conceptembedmodel_pa_k_kernel(tc, x, conv_w, conv_b, out):
 
         def transpose_and_quantise(raw_tile, first_pass_in_load, vector_helps, codes, scales):
             words = raw_tile[:].bitcast(F32)
-            grouped = stage.tile([P, GROUP * ROWS * PACK], BF16, tag="grouped", align_bytes=64)
+            grouped = stage.tile([P, GROUP * ROWS * PACK], BF16, tag="grouped", align_bytes=256)
             grouped_words = grouped[:].bitcast(F32)
             for i in range(GROUP):
                 for half in range(ROWS // BANK_ROWS):
@@ -95,11 +96,11 @@ def tile_conceptembedmodel_pa_k_kernel(tc, x, conv_w, conv_b, out):
         def prepare(g):
             x_raw, w_raw = loaded[(g * GROUP) // LOAD_PASSES]
             first_pass_in_load = (g * GROUP) % LOAD_PASSES
-            x_codes = quantised.tile([P, GROUP * ROWS], U32, tag="x_codes", align_bytes=64)
-            x_scales = quantised.tile([P, GROUP * ROWS], U8, tag="x_scales", align_bytes=64)
+            x_codes = quantised.tile([P, GROUP * ROWS], U32, tag="x_codes", align_bytes=256)
+            x_scales = quantised.tile([P, GROUP * ROWS], U8, tag="x_scales", align_bytes=256)
             transpose_and_quantise(x_raw, first_pass_in_load, True, x_codes, x_scales)
-            w_codes = quantised.tile([P, GROUP * ROWS], U32, tag="w_codes", align_bytes=64)
-            w_scales = quantised.tile([P, GROUP * ROWS], U8, tag="w_scales", align_bytes=64)
+            w_codes = quantised.tile([P, GROUP * ROWS], U32, tag="w_codes", align_bytes=256)
+            w_scales = quantised.tile([P, GROUP * ROWS], U8, tag="w_scales", align_bytes=256)
             transpose_and_quantise(w_raw, first_pass_in_load, False, w_codes, w_scales)
             return x_codes, x_scales, w_codes, w_scales
 
@@ -139,19 +140,20 @@ def tile_conceptembedmodel_pa_k_kernel(tc, x, conv_w, conv_b, out):
 
         mx_tiles = {}
         for g in range(GROUPS):
+            if g == BIAS_GROUP:
+                bias_rows_f32 = const.tile([P, P], F32)
+                nc.vector.tensor_copy(out=bias_rows_f32[:], in_=bias_rows[:])
             mx_tiles[g] = prepare(g)
             last_group_of_load = (g + 1) * GROUP % LOAD_PASSES == 0
             next_load = (g * GROUP) // LOAD_PASSES + RAW_BUFS
             if last_group_of_load and next_load < LOADS:
                 loaded[next_load] = load(next_load)
-            if g == 0:
-                bias_rows_f32 = const.tile([P, P], F32)
-                nc.vector.tensor_copy(out=bias_rows_f32[:], in_=bias_rows[:])
+            if g == BIAS_GROUP:
                 bias_bank = t_banks.tile([P, 2, BANK_ROWS], F32, tag="bank")
                 nc.tensor.transpose(out=bias_bank[:, 0, 0:P], in_=bias_rows_f32[:], identity=identity[:])
                 bias = const.tile([P, D_TILES], F32)
                 nc.vector.tensor_copy(out=bias[:], in_=bias_bank[:, 0, 0:D_TILES])
-            else:
+            if g > 0:
                 multiply(g - 1, mx_tiles[g - 1])
         multiply(GROUPS - 1, mx_tiles[GROUPS - 1])
 

@@ -26,7 +26,9 @@ GROUPS = PASSES // GROUP
 LOAD_PASSES = 2
 LOAD_K = LOAD_PASSES * K_PASS
 LOADS = PASSES // LOAD_PASSES
-BIAS_GROUP = 4
+WARM_START = 8
+WARM_GAP = 2
+WARM_GROUPS = 2
 RAW_BUFS = 6
 
 BANK_WORDS = 512
@@ -93,15 +95,23 @@ def tile_conceptembedmodel_pa_k_kernel(tc, x, conv_w, conv_b, out):
                     in_=grouped[:, i * ROWS * PACK : (i + 1) * ROWS * PACK],
                 )
 
+        def keep_warm(count):
+            for i in range(count):
+                nc.tensor.matmul(z[0][:], lhsT=zeros[:, 0:P], rhs=zeros[:], start=True, stop=True)
+
         def prepare(g):
             x_raw, w_raw = loaded[(g * GROUP) // LOAD_PASSES]
             first_pass_in_load = (g * GROUP) % LOAD_PASSES
             x_codes = quantised.tile([P, GROUP * ROWS], U32, tag="x_codes", align_bytes=256)
             x_scales = quantised.tile([P, GROUP * ROWS], U8, tag="x_scales", align_bytes=256)
             transpose_and_quantise(x_raw, first_pass_in_load, True, x_codes, x_scales)
+            if g < WARM_GROUPS:
+                keep_warm(WARM_GAP)
             w_codes = quantised.tile([P, GROUP * ROWS], U32, tag="w_codes", align_bytes=256)
             w_scales = quantised.tile([P, GROUP * ROWS], U8, tag="w_scales", align_bytes=256)
             transpose_and_quantise(w_raw, first_pass_in_load, False, w_codes, w_scales)
+            if g < WARM_GROUPS - 1:
+                keep_warm(WARM_GAP)
             return x_codes, x_scales, w_codes, w_scales
 
         def multiply(g, mx_tiles):
@@ -127,68 +137,53 @@ def tile_conceptembedmodel_pa_k_kernel(tc, x, conv_w, conv_b, out):
 
         identity = const.tile([P, P], F32)
         make_identity(nc, identity[:])
-        bias_rows = const.tile([P, P], BF16)
-        nc.vector.memset(bias_rows[:], 0.0)
-        nc.scalar.dma_start(out=bias_rows[0:D_TILES, :], in_=conv_b.rearrange("(m d) -> m d", m=D_TILES))
+        zeros = const.tile([P, ROWS], BF16)
+        nc.vector.memset(zeros[:], 0.0)
         warm = const.tile([P, 1], F32)
         nc.vector.memset(warm[:], 0.0)
         nc.scalar.activation(out=warm[:], in_=warm[:], func=mybir.ActivationFunctionType.Exp)
-        result = const.tile([P, P], F32)
-        nc.vector.memset(result[:], 0.0)
+        z_max = const.tile([P, P], F32)
+        nc.vector.memset(z_max[:], 0.0)
 
         z = [z_banks.tile([P, ROWS], F32, name="z%d" % m) for m in range(D_TILES)]
 
+        keep_warm(WARM_START)
         mx_tiles = {}
         for g in range(GROUPS):
-            if g == BIAS_GROUP:
-                bias_rows_f32 = const.tile([P, P], F32)
-                nc.vector.tensor_copy(out=bias_rows_f32[:], in_=bias_rows[:])
             mx_tiles[g] = prepare(g)
             last_group_of_load = (g + 1) * GROUP % LOAD_PASSES == 0
             next_load = (g * GROUP) // LOAD_PASSES + RAW_BUFS
             if last_group_of_load and next_load < LOADS:
                 loaded[next_load] = load(next_load)
-            if g == BIAS_GROUP:
-                bias_bank = t_banks.tile([P, 2, BANK_ROWS], F32, tag="bank")
-                nc.tensor.transpose(out=bias_bank[:, 0, 0:P], in_=bias_rows_f32[:], identity=identity[:])
-                bias = const.tile([P, D_TILES], F32)
-                nc.vector.tensor_copy(out=bias[:], in_=bias_bank[:, 0, 0:D_TILES])
             if g > 0:
                 multiply(g - 1, mx_tiles[g - 1])
         multiply(GROUPS - 1, mx_tiles[GROUPS - 1])
 
-        z_max = const.tile([P, SEQS * D_TILES], F32)
+        bias_rows = const.tile([SEQS * D_TILES, P], BF16)
+        for b in range(SEQS):
+            nc.sync.dma_start(
+                out=bias_rows[b * D_TILES : (b + 1) * D_TILES, :], in_=conv_b.rearrange("(m d) -> m d", m=D_TILES)
+            )
+
         for m in range(D_TILES):
             nc.vector.tensor_reduce(
-                out=z_max[:].rearrange("p (b m) -> p b m", m=D_TILES)[:, :, m],
+                out=z_max[:, 0 : SEQS * D_TILES].rearrange("p (b m) -> p b m", m=D_TILES)[:, :, m],
                 in_=z[m][:].rearrange("p (b l) -> p b l", l=POSITIONS),
                 axis=mybir.AxisListType.X,
                 op=ALU.max,
             )
-        v = const.tile([P, SEQS * D_TILES], F32)
-        nc.vector.tensor_tensor(
-            out=v[:].rearrange("p (b m) -> p b m", m=D_TILES),
-            in0=z_max[:].rearrange("p (b m) -> p b m", m=D_TILES),
-            in1=bias[:].unsqueeze(1).to_broadcast([P, SEQS, D_TILES]),
-            op=ALU.add,
-        )
-        negative = const.tile([P, SEQS * D_TILES], F32)
+        max_bank = t_banks.tile([P, 2, BANK_ROWS], F32, tag="bank")
+        nc.tensor.transpose(out=max_bank[:, 0, 0:P], in_=z_max[:], identity=identity[:])
+        v = const.tile([SEQS * D_TILES, P], F32)
+        nc.vector.tensor_tensor(out=v[:], in0=max_bank[0 : SEQS * D_TILES, 0, 0:P], in1=bias_rows[:], op=ALU.add)
+        negative = const.tile([SEQS * D_TILES, P], F32)
         nc.vector.tensor_scalar_min(out=negative[:], in0=v[:], scalar1=0.0)
-        exp_negative = const.tile([P, SEQS * D_TILES], F32)
+        exp_negative = const.tile([SEQS * D_TILES, P], F32)
         nc.scalar.activation(out=exp_negative[:], in_=negative[:], func=mybir.ActivationFunctionType.Exp)
-        positive = const.tile([P, SEQS * D_TILES], F32)
+        positive = const.tile([SEQS * D_TILES, P], F32)
         nc.vector.tensor_scalar_max(out=positive[:], in0=v[:], scalar1=0.0)
-        nc.vector.scalar_tensor_tensor(
-            out=result[:, 0 : SEQS * D_TILES],
-            in0=exp_negative[:],
-            scalar=-1.0,
-            in1=positive[:],
-            op0=ALU.add,
-            op1=ALU.add,
-        )
-
-        result_bank = t_banks.tile([P, 2, BANK_ROWS], F32, tag="bank")
-        nc.tensor.transpose(out=result_bank[:, 0, 0:P], in_=result[:], identity=identity[:])
         out_rows = const.tile([SEQS * D_TILES, P], F32)
-        nc.vector.tensor_copy(out=out_rows[:], in_=result_bank[0 : SEQS * D_TILES, 0, 0:P])
+        nc.vector.scalar_tensor_tensor(
+            out=out_rows[:], in0=exp_negative[:], scalar=-1.0, in1=positive[:], op0=ALU.add, op1=ALU.add
+        )
         nc.sync.dma_start(out=out.rearrange("b (m d) -> (b m) d", m=D_TILES), in_=out_rows[:])

@@ -26,9 +26,8 @@ GROUPS = PASSES // GROUP
 LOAD_PASSES = 2
 LOAD_K = LOAD_PASSES * K_PASS
 LOADS = PASSES // LOAD_PASSES
-WARM_START = 8
-WARM_GAP = 2
-WARM_GROUPS = 2
+KEPT_TILES = D_TILES - 1
+T_BANKS = 5
 RAW_BUFS = 6
 
 BANK_WORDS = 512
@@ -51,7 +50,7 @@ def tile_conceptembedmodel_pa_k_kernel(tc, x, conv_w, conv_b, out):
         stage = ctx.enter_context(tc.tile_pool(name="stage", bufs=3))
         quantised = ctx.enter_context(tc.tile_pool(name="quantised", bufs=2))
         z_banks = ctx.enter_context(tc.psum_pool(name="z_banks", bufs=1))
-        t_banks = ctx.enter_context(tc.psum_pool(name="t_banks", bufs=4))
+        t_banks = ctx.enter_context(tc.psum_pool(name="t_banks", bufs=T_BANKS))
 
         def load(i):
             features = slice(i * LOAD_K, (i + 1) * LOAD_K)
@@ -95,41 +94,40 @@ def tile_conceptembedmodel_pa_k_kernel(tc, x, conv_w, conv_b, out):
                     in_=grouped[:, i * ROWS * PACK : (i + 1) * ROWS * PACK],
                 )
 
-        def keep_warm(count):
-            for i in range(count):
-                nc.tensor.matmul(z[0][:], lhsT=zeros[:, 0:P], rhs=zeros[:], start=True, stop=True)
-
         def prepare(g):
             x_raw, w_raw = loaded[(g * GROUP) // LOAD_PASSES]
             first_pass_in_load = (g * GROUP) % LOAD_PASSES
             x_codes = quantised.tile([P, GROUP * ROWS], U32, tag="x_codes", align_bytes=256)
             x_scales = quantised.tile([P, GROUP * ROWS], U8, tag="x_scales", align_bytes=256)
             transpose_and_quantise(x_raw, first_pass_in_load, True, x_codes, x_scales)
-            if g < WARM_GROUPS:
-                keep_warm(WARM_GAP)
             w_codes = quantised.tile([P, GROUP * ROWS], U32, tag="w_codes", align_bytes=256)
             w_scales = quantised.tile([P, GROUP * ROWS], U8, tag="w_scales", align_bytes=256)
             transpose_and_quantise(w_raw, first_pass_in_load, False, w_codes, w_scales)
-            if g < WARM_GROUPS - 1:
-                keep_warm(WARM_GAP)
             return x_codes, x_scales, w_codes, w_scales
 
         def multiply(g, mx_tiles):
             x_codes, x_scales, w_codes, w_scales = mx_tiles
-            for m in range(D_TILES):
+            z_last = t_banks.tile([P, ROWS], F32, tag="bank")
+            kept = list(range(KEPT_TILES))
+            for m in kept + [KEPT_TILES] if g < GROUPS - 1 else [KEPT_TILES] + kept:
                 for i in range(GROUP):
                     c = g * GROUP + i
+                    is_kept = m < KEPT_TILES
                     x_cols = slice(i * ROWS, (i + 1) * ROWS)
                     w_cols = slice(i * ROWS + m * P, i * ROWS + (m + 1) * P)
                     nc.tensor.matmul_mx(
-                        out=z[m][:],
+                        out=z[m][:] if is_kept else z_last[:],
                         lhsT=w_codes[:, w_cols].bitcast(FP8X4),
                         lhsT_scale=w_scales[:, w_cols],
                         rhs=x_codes[:, x_cols].bitcast(FP8X4),
                         rhs_scale=x_scales[:, x_cols],
-                        start=(c == 0),
-                        stop=(c == PASSES - 1),
+                        start=(c == 0 if is_kept else i == 0),
+                        stop=(c == PASSES - 1 if is_kept else i == GROUP - 1),
                     )
+            if g == 0:
+                nc.vector.tensor_copy(out=last_sum[:], in_=z_last[:])
+            else:
+                nc.vector.tensor_tensor(out=last_sum[:], in0=z_last[:], in1=last_sum[:], op=ALU.add)
 
         loaded = {}
         for i in range(RAW_BUFS):
@@ -137,17 +135,15 @@ def tile_conceptembedmodel_pa_k_kernel(tc, x, conv_w, conv_b, out):
 
         identity = const.tile([P, P], F32)
         make_identity(nc, identity[:])
-        zeros = const.tile([P, ROWS], BF16)
-        nc.vector.memset(zeros[:], 0.0)
         warm = const.tile([P, 1], F32)
         nc.vector.memset(warm[:], 0.0)
         nc.scalar.activation(out=warm[:], in_=warm[:], func=mybir.ActivationFunctionType.Exp)
         z_max = const.tile([P, P], F32)
         nc.vector.memset(z_max[:], 0.0)
 
-        z = [z_banks.tile([P, ROWS], F32, name="z%d" % m) for m in range(D_TILES)]
+        z = [z_banks.tile([P, ROWS], F32, name="z%d" % m) for m in range(KEPT_TILES)]
+        last_sum = const.tile([P, ROWS], F32)
 
-        keep_warm(WARM_START)
         mx_tiles = {}
         for g in range(GROUPS):
             mx_tiles[g] = prepare(g)
@@ -165,10 +161,11 @@ def tile_conceptembedmodel_pa_k_kernel(tc, x, conv_w, conv_b, out):
                 out=bias_rows[b * D_TILES : (b + 1) * D_TILES, :], in_=conv_b.rearrange("(m d) -> m d", m=D_TILES)
             )
 
-        for m in range(D_TILES):
+        for m in [KEPT_TILES] + list(range(KEPT_TILES)):
+            sums = z[m] if m < KEPT_TILES else last_sum
             nc.vector.tensor_reduce(
                 out=z_max[:, 0 : SEQS * D_TILES].rearrange("p (b m) -> p b m", m=D_TILES)[:, :, m],
-                in_=z[m][:].rearrange("p (b l) -> p b l", l=POSITIONS),
+                in_=sums[:].rearrange("p (b l) -> p b l", l=POSITIONS),
                 axis=mybir.AxisListType.X,
                 op=ALU.max,
             )

from contextlib import ExitStack

import concourse.mybir as mybir
from concourse.masks import make_identity

F32 = mybir.dt.float32
BF16 = mybir.dt.bfloat16
U32 = mybir.dt.uint32
U8 = mybir.dt.uint8
FP8X4 = mybir.dt.float8_e4m3fn_x4
ALU = mybir.AluOpType

P = 128
PACK = 4
K_PASS = P * PACK
WORDS_PASS = K_PASS // 2

SEQS, POSITIONS, FEATURES, D_OUT = 16, 32, 16384, 512
ROWS = SEQS * POSITIONS
ROW_TILES = ROWS // P
D_TILES = D_OUT // P
PASSES = FEATURES // K_PASS

GROUP = 2
GROUPS = PASSES // GROUP
LOAD_PASSES = 2
LOAD_K = LOAD_PASSES * K_PASS
LOADS = PASSES // LOAD_PASSES
KEPT_TILES = D_TILES - 1
T_BANKS = 5
RAW_BUFS = 6

BANK_WORDS = 512
BANK_ROWS = BANK_WORDS // 2

FLOPS = 2 * ROWS * D_OUT * FEATURES

assert ROWS == D_OUT and LOAD_PASSES % GROUP == 0


def tile_conceptembedmodel_pa_k_kernel(tc, x, conv_w, conv_b, out):
    nc = tc.nc
    x_rows = x.rearrange("b l f -> (b l) f").rearrange("(t p) f -> p t f", p=P)
    w_rows = conv_w.rearrange("(t p) f -> p t f", p=P)

    with ExitStack() as ctx:
        ctx.enter_context(tc.manual_schedule())
        const = ctx.enter_context(tc.tile_pool(name="const", bufs=1))
        raw = ctx.enter_context(tc.tile_pool(name="raw", bufs=RAW_BUFS))
        stage = ctx.enter_context(tc.tile_pool(name="stage", bufs=3))
        quantised = ctx.enter_context(tc.tile_pool(name="quantised", bufs=2))
        z_banks = ctx.enter_context(tc.psum_pool(name="z_banks", bufs=1))
        t_banks = ctx.enter_context(tc.psum_pool(name="t_banks", bufs=T_BANKS))

        def load(i):
            features = slice(i * LOAD_K, (i + 1) * LOAD_K)
            x_raw = raw.tile([P, ROW_TILES * LOAD_K], BF16, tag="x_raw")
            nc.sync.dma_start(
                out=x_raw[:].rearrange("p (t k) -> p t k", t=ROW_TILES), in_=x_rows[:, :, features]
            )
            w_raw = raw.tile([P, ROW_TILES * LOAD_K], BF16, tag="w_raw")
            nc.sync.dma_start(
                out=w_raw[:].rearrange("p (t k) -> p t k", t=ROW_TILES), in_=w_rows[:, :, features]
            )
            return x_raw, w_raw

        def transpose_and_quantise(raw_tile, first_pass_in_load, vector_helps, codes, scales):
            words = raw_tile[:].bitcast(F32)
            grouped = stage.tile([P, GROUP * ROWS * PACK], BF16, tag="grouped", align_bytes=256)
            grouped_words = grouped[:].bitcast(F32)
            for i in range(GROUP):
                for half in range(ROWS // BANK_ROWS):
                    bank = t_banks.tile([P, 2, BANK_ROWS], F32, tag="bank")
                    for u in range(2):
                        for j in range(BANK_ROWS // P):
                            t = half * (BANK_ROWS // P) + j
                            first_word = t * (LOAD_K // 2) + (first_pass_in_load + i) * WORDS_PASS + u * P
                            nc.tensor.transpose(
                                out=bank[:, u, j * P : (j + 1) * P],
                                in_=words[:, first_word : first_word + P],
                                identity=identity[:],
                            )
                    first = (i * ROWS + half * BANK_ROWS) * 2
                    side_by_side = grouped_words[:, first : first + BANK_WORDS].rearrange("p (r u) -> p r u", u=2)
                    planes = bank[:].rearrange("p u r -> p r u")
                    if vector_helps and half == 1:
                        nc.vector.tensor_copy(out=side_by_side, in_=planes)
                    else:
                        nc.scalar.copy(out=side_by_side, in_=planes)
            for i in range(GROUP):
                nc.vector.quantize_mx(
                    out=codes[:, i * ROWS : (i + 1) * ROWS].bitcast(FP8X4),
                    scales=scales[:, i * ROWS : (i + 1) * ROWS],
                    in_=grouped[:, i * ROWS * PACK : (i + 1) * ROWS * PACK],
                )

        def prepare(g):
            x_raw, w_raw = loaded[(g * GROUP) // LOAD_PASSES]
            first_pass_in_load = (g * GROUP) % LOAD_PASSES
            x_codes = quantised.tile([P, GROUP * ROWS], U32, tag="x_codes", align_bytes=256)
            x_scales = quantised.tile([P, GROUP * ROWS], U8, tag="x_scales", align_bytes=256)
            transpose_and_quantise(x_raw, first_pass_in_load, True, x_codes, x_scales)
            w_codes = quantised.tile([P, GROUP * ROWS], U32, tag="w_codes", align_bytes=256)
            w_scales = quantised.tile([P, GROUP * ROWS], U8, tag="w_scales", align_bytes=256)
            transpose_and_quantise(w_raw, first_pass_in_load, False, w_codes, w_scales)
            return x_codes, x_scales, w_codes, w_scales

        def multiply(g, mx_tiles):
            x_codes, x_scales, w_codes, w_scales = mx_tiles
            z_last = t_banks.tile([P, ROWS], F32, tag="bank")
            kept = list(range(KEPT_TILES))
            for m in kept + [KEPT_TILES] if g < GROUPS - 1 else [KEPT_TILES] + kept:
                for i in range(GROUP):
                    c = g * GROUP + i
                    is_kept = m < KEPT_TILES
                    x_cols = slice(i * ROWS, (i + 1) * ROWS)
                    w_cols = slice(i * ROWS + m * P, i * ROWS + (m + 1) * P)
                    nc.tensor.matmul_mx(
                        out=z[m][:] if is_kept else z_last[:],
                        lhsT=w_codes[:, w_cols].bitcast(FP8X4),
                        lhsT_scale=w_scales[:, w_cols],
                        rhs=x_codes[:, x_cols].bitcast(FP8X4),
                        rhs_scale=x_scales[:, x_cols],
                        start=(c == 0 if is_kept else i == 0),
                        stop=(c == PASSES - 1 if is_kept else i == GROUP - 1),
                    )
            if g == 0:
                nc.vector.tensor_copy(out=last_sum[:], in_=z_last[:])
            else:
                nc.vector.tensor_tensor(out=last_sum[:], in0=z_last[:], in1=last_sum[:], op=ALU.add)

        loaded = {}
        for i in range(RAW_BUFS):
            loaded[i] = load(i)

        identity = const.tile([P, P], F32)
        make_identity(nc, identity[:])
        warm = const.tile([P, 1], F32)
        nc.vector.memset(warm[:], 0.0)
        nc.scalar.activation(out=warm[:], in_=warm[:], func=mybir.ActivationFunctionType.Exp)
        z_max = const.tile([P, P], F32)
        nc.vector.memset(z_max[:], 0.0)

        z = [z_banks.tile([P, ROWS], F32, name="z%d" % m) for m in range(KEPT_TILES)]
        last_sum = const.tile([P, ROWS], F32)

        mx_tiles = {}
        for g in range(GROUPS):
            mx_tiles[g] = prepare(g)
            last_group_of_load = (g + 1) * GROUP % LOAD_PASSES == 0
            next_load = (g * GROUP) // LOAD_PASSES + RAW_BUFS
            if last_group_of_load and next_load < LOADS:
                loaded[next_load] = load(next_load)
            if g > 0:
                multiply(g - 1, mx_tiles[g - 1])
        multiply(GROUPS - 1, mx_tiles[GROUPS - 1])

        bias_rows = const.tile([SEQS * D_TILES, P], BF16)
        for b in range(SEQS):
            nc.sync.dma_start(
                out=bias_rows[b * D_TILES : (b + 1) * D_TILES, :], in_=conv_b.rearrange("(m d) -> m d", m=D_TILES)
            )

        for m in [KEPT_TILES] + list(range(KEPT_TILES)):
            sums = z[m] if m < KEPT_TILES else last_sum
            nc.vector.tensor_reduce(
                out=z_max[:, 0 : SEQS * D_TILES].rearrange("p (b m) -> p b m", m=D_TILES)[:, :, m],
                in_=sums[:].rearrange("p (b l) -> p b l", l=POSITIONS),
                axis=mybir.AxisListType.X,
                op=ALU.max,
            )
        max_bank = t_banks.tile([P, 2, BANK_ROWS], F32, tag="bank")
        nc.tensor.transpose(out=max_bank[:, 0, 0:P], in_=z_max[:], identity=identity[:])
        v = const.tile([SEQS * D_TILES, P], F32)
        nc.vector.tensor_tensor(out=v[:], in0=max_bank[0 : SEQS * D_TILES, 0, 0:P], in1=bias_rows[:], op=ALU.add)
        negative = const.tile([SEQS * D_TILES, P], F32)
        nc.vector.tensor_scalar_min(out=negative[:], in0=v[:], scalar1=0.0)
        exp_negative = const.tile([SEQS * D_TILES, P], F32)
        nc.scalar.activation(out=exp_negative[:], in_=negative[:], func=mybir.ActivationFunctionType.Exp)
        positive = const.tile([SEQS * D_TILES, P], F32)
        nc.vector.tensor_scalar_max(out=positive[:], in0=v[:], scalar1=0.0)
        out_rows = const.tile([SEQS * D_TILES, P], F32)
        nc.vector.scalar_tensor_tensor(
            out=out_rows[:], in0=exp_negative[:], scalar=-1.0, in1=positive[:], op0=ALU.add, op1=ALU.add
        )
        nc.sync.dma_start(out=out.rearrange("b (m d) -> (b m) d", m=D_TILES), in_=out_rows[:])
